import numpy as np
import ml_dtypes


def mxq(x, axis, fmt="e4m3"):
    dtype, down = {"e4m3": (ml_dtypes.float8_e4m3fn, 7), "e5m2": (ml_dtypes.float8_e5m2, 14)}[fmt]
    v = np.moveaxis(np.asarray(x, np.float32).astype(ml_dtypes.bfloat16).astype(np.float64), axis, -1)
    blocks = v.reshape(v.shape[:-1] + (-1, 32))
    amax = np.abs(blocks).max(-1, keepdims=True)
    byte = np.maximum(np.where(amax > 0, np.frexp(amax)[1] - 1 + 127, 0) - down, 1)
    scale = np.exp2(byte - 127.0)
    codes = (blocks / scale).astype(np.float32).astype(dtype).astype(np.float64)
    return np.moveaxis((codes * scale).reshape(v.shape), -1, axis)


WIDE = False


def mx_kscale(k):
    if not WIDE:
        return np.ones(k)
    levels = np.array([10, -10, 5, -5, 0])
    if k % 512:
        return np.exp2(np.random.permutation(np.resize(levels, k // 32))).repeat(32)
    a = np.empty((k // 512, 16))
    for p in range(k // 512):
        a[p, :8] = np.random.permutation(np.resize(levels, 8))
        for g in range(8):
            far = levels[np.abs(levels - a[p, g]) >= 10]
            a[p, g + 8] = far[np.random.randint(len(far))]
    return np.exp2(a.ravel()).repeat(32)


BF16 = ml_dtypes.bfloat16


def bf(x):
    return np.asarray(x, np.float32).astype(BF16)


def f64(x):
    return np.asarray(x).astype(np.float64)


B, D, U1, U2 = 256, 8192, 512, 256
THRESHOLD = 1.0


def setup_inputs():
    s, t = mx_kscale(D), mx_kscale(U1)
    c = s / s.mean()
    u = np.random.random(B)
    target = np.where(np.random.random(B) < 0.5, 0.5 + 0.35 * u, 1.15 + 0.45 * u)
    g = np.random.standard_normal((B, D)) * c
    x = g * (target / np.mean(np.abs(g), axis=1))[:, None]
    return {"x": bf(x),
            "W1": bf(np.random.standard_normal((U1, D)) / np.sqrt(D) / c[None, :] * t[:, None]),
            "b1": bf(np.random.standard_normal(U1) * 0.3 * t),
            "W2": bf(np.random.standard_normal((U2, D)) / np.sqrt(D) / c[None, :] * t[:U2, None]),
            "b2": bf(np.random.standard_normal(U2) * 0.3 * t[:U2]),
            "Wf": bf(np.random.standard_normal((D, U1)) * 1.5 / np.sqrt(U1) / t[None, :]),
            "bf": bf(np.random.standard_normal(D) * 0.3)}


def reference(x, W1, b1, W2, b2, Wf, bf):
    x = f64(x)
    mask = np.mean(np.abs(x), axis=1) > THRESHOLD
    xq = mxq(x, 1, "e4m3")
    o1 = np.maximum((xq @ mxq(f64(W1), 1, "e4m3").T) + f64(b1), 0.0)
    o2 = np.maximum((xq @ mxq(f64(W2), 1, "e4m3").T) + f64(b2), 0.0)
    final_dim = W1.shape[0]
    o2p = np.pad(o2, ((0, 0), (0, final_dim - o2.shape[1])))
    branch_out = np.where(mask[:, None], o1, o2p)
    return (mxq(branch_out, 1, "e4m3") @ mxq(f64(Wf), 1, "e4m3").T) + f64(bf)

@@ -1,0 +1,305 @@
+from contextlib import ExitStack
+
+import concourse.mybir as mybir
+from concourse.masks import make_identity
+
+F32 = mybir.dt.float32
+BF16 = mybir.dt.bfloat16
+U32 = mybir.dt.uint32
+U8 = mybir.dt.uint8
+FP8X4 = mybir.dt.float8_e4m3fn_x4
+ALU = mybir.AluOpType
+ACT = mybir.ActivationFunctionType
+AX = mybir.AxisListType
+
+B, D, U1, U2 = 256, 8192, 512, 256
+THRESHOLD = 1.0
+FLOPS = 2 * B * D * (U1 + U2) + 2 * B * U1 * D
+
+P = 128
+K_PASS = 512
+PASS_WORDS = K_PASS // 2
+PASSES = D // K_PASS
+BANKS = 4
+GROUP_COLS = 1024
+GROUP_ELEMS = 4 * GROUP_COLS
+X_GROUPS = B * PASSES // GROUP_COLS
+W_CHUNKS = (U1 + U2) // B
+CHUNK_GROUPS = PASSES // BANKS
+F_GROUPS = D // GROUP_COLS
+N_OUT = 512
+ABS_PIECES = 16
+ABS_COLS = 2 * D // ABS_PIECES
+
+
+def tile_dynamiclayer_k_kernel(tc, x, W1, b1, W2, b2, Wf, bf, out):
+    nc = tc.nc
+    with ExitStack() as ctx:
+        ctx.enter_context(tc.manual_schedule())
+        keep = ctx.enter_context(tc.tile_pool(name="keep", bufs=1))
+        x_pool = ctx.enter_context(tc.tile_pool(name="x_pool", bufs=X_GROUPS))
+        w_pool = ctx.enter_context(tc.tile_pool(name="w_pool", bufs=8))
+        grouped_pool = ctx.enter_context(tc.tile_pool(name="grouped_pool", bufs=3))
+        codes_pool = ctx.enter_context(tc.tile_pool(name="codes_pool", bufs=3))
+        scratch_pool = ctx.enter_context(tc.tile_pool(name="scratch_pool", bufs=2))
+        part_pool = ctx.enter_context(tc.tile_pool(name="part_pool", bufs=2))
+        out_pool = ctx.enter_context(tc.tile_pool(name="out_pool", bufs=4))
+        psum = ctx.enter_context(tc.psum_pool(name="psum", bufs=6))
+        sums_pool = ctx.enter_context(tc.psum_pool(name="sums_pool", bufs=2))
+
+        x_rows = []
+        for g in range(X_GROUPS):
+            cols = slice(g * GROUP_ELEMS // 2, (g + 1) * GROUP_ELEMS // 2)
+            rows = x_pool.tile([P, GROUP_ELEMS], BF16, tag="x_rows")
+            nc.sync.dma_start(
+                out=rows[:].rearrange("p (t k) -> p t k", t=2),
+                in_=x[:, cols].rearrange("(t p) k -> p t k", p=P),
+            )
+            x_rows.append(rows)
+
+        w_views = [W2, W1[0:B, :], W1[B : 2 * B, :]]
+        w_rows = []
+        for n, view in enumerate(w_views):
+            halves = []
+            for half in range(2):
+                pair = []
+                for a in range(2):
+                    rows = w_pool.tile([P, GROUP_ELEMS], BF16, tag="rows")
+                    nc.sync.dma_start(
+                        out=rows[:],
+                        in_=view[a * P : (a + 1) * P, half * GROUP_ELEMS : (half + 1) * GROUP_ELEMS],
+                    )
+                    pair.append(rows)
+                halves.append(pair)
+            w_rows.append(halves)
+            if n == 0:
+                bias2 = keep.tile([P, U2], BF16)
+                nc.sync.dma_start(out=bias2[:], in_=b2.partition_broadcast(P))
+                bias1 = keep.tile([P, U1], BF16)
+                nc.sync.dma_start(out=bias1[:], in_=b1.partition_broadcast(P))
+        bias = keep.tile([P, D], BF16)
+        nc.sync.dma_start(out=bias[:], in_=bf.partition_broadcast(P))
+        f_rows = []
+        for c in range(F_GROUPS):
+            rows = w_pool.tile([P, GROUP_ELEMS], BF16, tag="rows")
+            nc.sync.dma_start(
+                out=rows[:],
+                in_=Wf[c * GROUP_COLS : (c + 1) * GROUP_COLS, :].rearrange("(p n) k -> p (n k)", p=P),
+            )
+            f_rows.append(rows)
+
+        ident_f32 = keep.tile([P, P], F32)
+        make_identity(nc, ident_f32[:])
+
+        x_codes = keep.tile([P, PASSES * B], U32, align_bytes=64)
+        x_scales = keep.tile([P, PASSES * B], U8, align_bytes=64)
+        abs_sums = keep.tile([P, 2, ABS_PIECES // 2], F32)
+        takes = keep.tile([P, 2, 2], F32)
+        h_grouped = keep.tile([P, 4 * B], BF16, align_bytes=64)
+        h_codes = keep.tile([P, B], U32, align_bytes=64)
+        h_scales = keep.tile([P, B], U8, align_bytes=64)
+        h_rows = [keep.tile([P, U1], BF16, name="h_rows_%d" % t) for t in range(2)]
+
+        def turned_group(blocks, rows_first, vector_banks, codes, scales):
+            made = {}
+
+            def turn():
+                banks = []
+                for i in range(BANKS):
+                    bank = psum.tile([P, 4, P], F32, tag="bank")
+                    for s in range(4):
+                        nc.tensor.transpose(bank[:, s, :], blocks[4 * i + s], ident_f32[:])
+                    banks.append(bank)
+                grouped = grouped_pool.tile([P, GROUP_ELEMS], BF16, tag="grouped", align_bytes=64)
+                words = grouped[:].bitcast(F32)
+                for i in range(BANKS):
+                    if rows_first:
+                        dst = words.rearrange("p (r i a u) -> p i r a u", i=BANKS, a=2, u=2)[:, i]
+                        src = banks[i][:].rearrange("p (a u) r -> p r a u", u=2)
+                    else:
+                        dst = words.rearrange("p (i a r u) -> p i a r u", i=BANKS, a=2, u=2)[:, i]
+                        src = banks[i][:].rearrange("p (a u) r -> p a r u", u=2)
+                    if i < vector_banks:
+                        nc.vector.tensor_copy(out=dst, in_=src)
+                    else:
+                        nc.scalar.copy(out=dst, in_=src)
+                made["grouped"] = grouped
+
+            def quantise():
+                nc.vector.quantize_mx(out=codes.bitcast(FP8X4), scales=scales, in_=made["grouped"][:])
+
+            return turn, quantise
+
+        def sum_abs(piece):
+            g, quarter = piece // 4, piece % 4
+            scratch = scratch_pool.tile([P, ABS_COLS], BF16, tag="scratch")
+            nc.scalar.activation(
+                out=scratch[:],
+                in_=x_rows[g][:, quarter * ABS_COLS : (quarter + 1) * ABS_COLS],
+                func=ACT.Abs,
+                accum_out=abs_sums[:, quarter // 2, 2 * g + quarter % 2 : 2 * g + quarter % 2 + 1],
+            )
+
+        def every_second(words, first):
+            return words[:, first:PASS_WORDS:2]
+
+        def nothing():
+            return None
+
+        pipeline = []
+
+        for g in range(X_GROUPS):
+            words = x_rows[g][:].bitcast(F32)
+            blocks = []
+            for i in range(BANKS):
+                for t in range(2):
+                    for u in range(2):
+                        blocks.append(every_second(words[:, t * GROUP_COLS + i * PASS_WORDS : t * GROUP_COLS + (i + 1) * PASS_WORDS], u))
+            cols = slice(g * GROUP_COLS, (g + 1) * GROUP_COLS)
+            turn, quantise = turned_group(blocks, False, 2, x_codes[:, cols], x_scales[:, cols])
+
+            def turn_x(g=g, turn=turn):
+                sum_abs(g)
+                turn()
+
+            pipeline.append((turn_x, quantise, nothing))
+
+        def compare_means():
+            mean_abs = keep.tile([P, 2], F32)
+            nc.vector.tensor_reduce(out=mean_abs[:], in_=abs_sums[:], axis=AX.X, op=ALU.add)
+            nc.vector.tensor_scalar(
+                out=takes[:, 0, :], in0=mean_abs[:], scalar1=1.0 / D, scalar2=THRESHOLD, op0=ALU.mult, op1=ALU.is_gt
+            )
+            nc.vector.tensor_scalar(
+                out=takes[:, 1, :], in0=mean_abs[:], scalar1=1.0 / D, scalar2=THRESHOLD, op0=ALU.mult, op1=ALU.is_le
+            )
+
+        biased2 = [keep.tile([P, B], F32, name="biased2_%d" % t) for t in range(2)]
+
+        def finish_chunk(n, sums):
+            if n == 0:
+                for t in range(2):
+                    nc.vector.tensor_tensor(out=biased2[t][:], in0=sums[t][:], in1=bias2[:], op=ALU.add)
+                return
+            if n == 1:
+                compare_means()
+            biased1 = [part_pool.tile([P, B], F32, name="biased1_%d" % t) for t in range(2)]
+            for t in range(2):
+                nc.vector.tensor_tensor(
+                    out=biased1[t][:], in0=sums[t][:], in1=bias1[:, (n - 1) * B : n * B], op=ALU.add
+                )
+            if n == 2:
+                for t in range(2):
+                    nc.scalar.activation(
+                        out=h_rows[t][:, B:], in_=biased1[t][:], func=ACT.Relu, scale=takes[:, 0, t : t + 1]
+                    )
+                return
+            for t in range(2):
+                part1 = part_pool.tile([P, B], BF16, tag="part1")
+                part2 = part_pool.tile([P, B], BF16, tag="part2")
+                nc.scalar.activation(out=part1[:], in_=biased1[t][:], func=ACT.Relu, scale=takes[:, 0, t : t + 1])
+                nc.scalar.activation(out=part2[:], in_=biased2[t][:], func=ACT.Relu, scale=takes[:, 1, t : t + 1])
+                nc.vector.tensor_tensor(out=h_rows[t][:, 0:B], in0=part1[:], in1=part2[:], op=ALU.add)
+
+        for n in range(W_CHUNKS):
+            open_sums = []
+            for q in range(CHUNK_GROUPS):
+                half, quarter = q // 2, q % 2
+                blocks = []
+                for i in range(BANKS):
+                    for a in range(2):
+                        first = (quarter * BANKS + i) * PASS_WORDS
+                        words = w_rows[n][half][a][:].bitcast(F32)[:, first : first + PASS_WORDS]
+                        for u in range(2):
+                            blocks.append(every_second(words, u))
+                codes = codes_pool.tile([P, GROUP_COLS], U32, tag="codes", align_bytes=64)
+                scales = codes_pool.tile([P, GROUP_COLS], U8, tag="scales", align_bytes=64)
+                turn, quantise = turned_group(blocks, False, 2, codes[:], scales[:])
+
+                def turn_w(w=n * CHUNK_GROUPS + q, turn=turn):
+                    if w < 6:
+                        sum_abs(X_GROUPS + 2 * w)
+                        sum_abs(X_GROUPS + 2 * w + 1)
+                    turn()
+
+                def multiply_w(n=n, q=q, codes=codes, scales=scales, open_sums=open_sums):
+                    for t in range(2):
+                        if q == 0:
+                            sums = sums_pool.tile([P, N_OUT], F32, tag="sums")
+                            open_sums.append(sums[:, 0:B])
+                        for j in range(BANKS):
+                            g = q * BANKS + j
+                            first = g * B + t * P
+                            nc.tensor.matmul_mx(
+                                out=open_sums[t],
+                                lhsT=x_codes[:, first : first + P].bitcast(FP8X4),
+                                lhsT_scale=x_scales[:, first : first + P],
+                                rhs=codes[:, j * B : (j + 1) * B].bitcast(FP8X4),
+                                rhs_scale=scales[:, j * B : (j + 1) * B],
+                                start=(g == 0),
+                                stop=(g == PASSES - 1),
+                            )
+                    if q == CHUNK_GROUPS - 1:
+                        finish_chunk(n, open_sums)
+
+                pipeline.append((turn_w, quantise, multiply_w))
+
+        def turn_h():
+            bank = psum.tile([P, 4, P], F32, tag="bank")
+            for t in range(2):
+                for u in range(2):
+                    nc.tensor.transpose(bank[:, 2 * t + u, :], every_second(h_rows[t][:].bitcast(F32), u), ident_f32[:])
+            nc.vector.tensor_copy(
+                out=h_grouped[:].bitcast(F32).rearrange("p (t r u) -> p t r u", t=2, u=2),
+                in_=bank[:].rearrange("p (t u) r -> p t r u", u=2),
+            )
+            nc.vector.quantize_mx(out=h_codes[:].bitcast(FP8X4), scales=h_scales[:], in_=h_grouped[:])
+
+        pipeline.append((nothing, nothing, turn_h))
+
+        for c in range(F_GROUPS):
+            words = f_rows[c][:].bitcast(F32)
+            blocks = [every_second(words[:, j * PASS_WORDS : (j + 1) * PASS_WORDS], u) for j in range(2 * BANKS) for u in range(2)]
+            codes = codes_pool.tile([P, GROUP_COLS], U32, tag="codes", align_bytes=64)
+            scales = codes_pool.tile([P, GROUP_COLS], U8, tag="scales", align_bytes=64)
+            turn, quantise = turned_group(blocks, True, 0, codes[:], scales[:])
+
+            def multiply_f(c=c, codes=codes, scales=scales):
+                for t in range(2):
+                    result = out_pool.tile([P, GROUP_COLS], F32, tag="result")
+                    for j in range(GROUP_COLS // N_OUT):
+                        cols = slice(j * N_OUT, (j + 1) * N_OUT)
+                        if j == 0:
+                            sums = sums_pool.tile([P, N_OUT], F32, tag="sums")
+                        else:
+                            sums = psum.tile([P, N_OUT], F32, tag="bank")
+                        nc.tensor.matmul_mx(
+                            out=sums[:],
+                            lhsT=h_codes[:, t * P : (t + 1) * P].bitcast(FP8X4),
+                            lhsT_scale=h_scales[:, t * P : (t + 1) * P],
+                            rhs=codes[:, cols].bitcast(FP8X4),
+                            rhs_scale=scales[:, cols],
+                            start=True,
+                            stop=True,
+                        )
+                        first = c * GROUP_COLS + j * N_OUT
+                        if t == 0 and j == 0:
+                            nc.scalar.copy(out=result[:, cols], in_=sums[:])
+                            nc.gpsimd.tensor_tensor(
+                                out=result[:, cols], in0=result[:, cols], in1=bias[:, first : first + N_OUT], op=ALU.add
+                            )
+                        else:
+                            nc.vector.tensor_tensor(
+                                out=result[:, cols], in0=sums[:], in1=bias[:, first : first + N_OUT], op=ALU.add
+                            )
+                    nc.sync.dma_start(out=out[t * P : (t + 1) * P, c * GROUP_COLS : (c + 1) * GROUP_COLS], in_=result[:])
+
+            pipeline.append((turn, quantise, multiply_f))
+
+        for i in range(len(pipeline) + 2):
+            if i < len(pipeline):
+                pipeline[i][0]()
+            if 1 <= i <= len(pipeline):
+                pipeline[i - 1][1]()
+            if i >= 2:
+                pipeline[i - 2][2]()

@@ -42,6 +42,7 @@ def tile_dynamiclayer_k_kernel(tc, x, W1, b1, W2, b2, Wf, bf, out):
         grouped_pool = ctx.enter_context(tc.tile_pool(name="grouped_pool", bufs=3))
         codes_pool = ctx.enter_context(tc.tile_pool(name="codes_pool", bufs=3))
         scratch_pool = ctx.enter_context(tc.tile_pool(name="scratch_pool", bufs=2))
+        sorted_pool = ctx.enter_context(tc.tile_pool(name="sorted_pool", bufs=2))
         part_pool = ctx.enter_context(tc.tile_pool(name="part_pool", bufs=2))
         out_pool = ctx.enter_context(tc.tile_pool(name="out_pool", bufs=4))
         psum = ctx.enter_context(tc.psum_pool(name="psum", bufs=6))
@@ -60,18 +61,14 @@ def tile_dynamiclayer_k_kernel(tc, x, W1, b1, W2, b2, Wf, bf, out):
         w_views = [W2, W1[0:B, :], W1[B : 2 * B, :]]
         w_rows = []
         for n, view in enumerate(w_views):
-            halves = []
-            for half in range(2):
-                pair = []
-                for a in range(2):
-                    rows = w_pool.tile([P, GROUP_ELEMS], BF16, tag="rows")
-                    nc.sync.dma_start(
-                        out=rows[:],
-                        in_=view[a * P : (a + 1) * P, half * GROUP_ELEMS : (half + 1) * GROUP_ELEMS],
-                    )
-                    pair.append(rows)
-                halves.append(pair)
-            w_rows.append(halves)
+            for q in range(CHUNK_GROUPS):
+                cols = slice(q * GROUP_ELEMS // 2, (q + 1) * GROUP_ELEMS // 2)
+                rows = w_pool.tile([P, GROUP_ELEMS], BF16, tag="rows")
+                nc.sync.dma_start(
+                    out=rows[:].rearrange("p (t k) -> p t k", t=2),
+                    in_=view[:, cols].rearrange("(t p) k -> p t k", p=P),
+                )
+                w_rows.append(rows)
             if n == 0:
                 bias2 = keep.tile([P, U2], BF16)
                 nc.sync.dma_start(out=bias2[:], in_=b2.partition_broadcast(P))
@@ -108,7 +105,7 @@ def tile_dynamiclayer_k_kernel(tc, x, W1, b1, W2, b2, Wf, bf, out):
                 for i in range(BANKS):
                     bank = psum.tile([P, 4, P], F32, tag="bank")
                     for s in range(4):
-                        nc.tensor.transpose(bank[:, s, :], blocks[4 * i + s], ident_f32[:])
+                        nc.tensor.transpose(bank[:, s, :], blocks()[4 * i + s], ident_f32[:])
                     banks.append(bank)
                 grouped = grouped_pool.tile([P, GROUP_ELEMS], BF16, tag="grouped", align_bytes=64)
                 words = grouped[:].bitcast(F32)
@@ -140,8 +137,40 @@ def tile_dynamiclayer_k_kernel(tc, x, W1, b1, W2, b2, Wf, bf, out):
                 accum_out=abs_sums[:, quarter // 2, 2 * g + quarter % 2 : 2 * g + quarter % 2 + 1],
             )
 
+        def presorted(rows):
+            made = {}
+
+            def sort():
+                by_parity = sorted_pool.tile([P, GROUP_ELEMS], BF16, tag="sorted")
+                nc.vector.tensor_copy(
+                    out=by_parity[:].bitcast(F32).rearrange("p (b u w) -> p b u w", u=2, w=P),
+                    in_=rows[:].bitcast(F32).rearrange("p (b w u) -> p b u w", u=2, w=P),
+                )
+                made["rows"] = by_parity
+
+            def blocks():
+                words = made["rows"][:].bitcast(F32)
+                return [
+                    words[:, ((a * BANKS + i) * 2 + u) * P : ((a * BANKS + i) * 2 + u + 1) * P]
+                    for i in range(BANKS)
+                    for a in range(2)
+                    for u in range(2)
+                ]
+
+            return sort, blocks
+
         def every_second(words, first):
             return words[:, first:PASS_WORDS:2]
+
+        def stepped(rows):
+            words = rows[:].bitcast(F32)
+            blocks = []
+            for i in range(BANKS):
+                for a in range(2):
+                    first = (a * BANKS + i) * PASS_WORDS
+                    for u in range(2):
+                        blocks.append(every_second(words[:, first : first + PASS_WORDS], u))
+            return lambda: blocks
 
         def nothing():
             return None
@@ -149,20 +178,14 @@ def tile_dynamiclayer_k_kernel(tc, x, W1, b1, W2, b2, Wf, bf, out):
         pipeline = []
 
         for g in range(X_GROUPS):
-            words = x_rows[g][:].bitcast(F32)
-            blocks = []
-            for i in range(BANKS):
-                for t in range(2):
-                    for u in range(2):
-                        blocks.append(every_second(words[:, t * GROUP_COLS + i * PASS_WORDS : t * GROUP_COLS + (i + 1) * PASS_WORDS], u))
             cols = slice(g * GROUP_COLS, (g + 1) * GROUP_COLS)
-            turn, quantise = turned_group(blocks, False, 2, x_codes[:, cols], x_scales[:, cols])
+            turn, quantise = turned_group(stepped(x_rows[g]), False, 2, x_codes[:, cols], x_scales[:, cols])
 
             def turn_x(g=g, turn=turn):
                 sum_abs(g)
                 turn()
 
-            pipeline.append((turn_x, quantise, nothing))
+            pipeline.append((nothing, turn_x, quantise, nothing))
 
         def compare_means():
             mean_abs = keep.tile([P, 2], F32)
@@ -174,52 +197,39 @@ def tile_dynamiclayer_k_kernel(tc, x, W1, b1, W2, b2, Wf, bf, out):
                 out=takes[:, 1, :], in0=mean_abs[:], scalar1=1.0 / D, scalar2=THRESHOLD, op0=ALU.mult, op1=ALU.is_le
             )
 
-        biased2 = [keep.tile([P, B], F32, name="biased2_%d" % t) for t in range(2)]
+        biased = [[keep.tile([P, B], F32, name="biased_%d_%d" % (n, t)) for t in range(2)] for n in range(W_CHUNKS)]
+        chunk_bias = [bias2[:], bias1[:, 0:B], bias1[:, B : 2 * B]]
 
         def finish_chunk(n, sums):
-            if n == 0:
-                for t in range(2):
-                    nc.vector.tensor_tensor(out=biased2[t][:], in0=sums[t][:], in1=bias2[:], op=ALU.add)
-                return
-            if n == 1:
-                compare_means()
-            biased1 = [part_pool.tile([P, B], F32, name="biased1_%d" % t) for t in range(2)]
             for t in range(2):
-                nc.vector.tensor_tensor(
-                    out=biased1[t][:], in0=sums[t][:], in1=bias1[:, (n - 1) * B : n * B], op=ALU.add
-                )
-            if n == 2:
-                for t in range(2):
+                nc.vector.tensor_tensor(out=biased[n][t][:], in0=sums[t], in1=chunk_bias[n], op=ALU.add)
+                if n == 2:
                     nc.scalar.activation(
-                        out=h_rows[t][:, B:], in_=biased1[t][:], func=ACT.Relu, scale=takes[:, 0, t : t + 1]
+                        out=h_rows[t][:, B:], in_=biased[n][t][:], func=ACT.Relu, scale=takes[:, 0, t : t + 1]
                     )
-                return
+
+        def select_first_half():
             for t in range(2):
                 part1 = part_pool.tile([P, B], BF16, tag="part1")
                 part2 = part_pool.tile([P, B], BF16, tag="part2")
-                nc.scalar.activation(out=part1[:], in_=biased1[t][:], func=ACT.Relu, scale=takes[:, 0, t : t + 1])
-                nc.scalar.activation(out=part2[:], in_=biased2[t][:], func=ACT.Relu, scale=takes[:, 1, t : t + 1])
+                nc.scalar.activation(out=part1[:], in_=biased[1][t][:], func=ACT.Relu, scale=takes[:, 0, t : t + 1])
+                nc.scalar.activation(out=part2[:], in_=biased[0][t][:], func=ACT.Relu, scale=takes[:, 1, t : t + 1])
                 nc.vector.tensor_tensor(out=h_rows[t][:, 0:B], in0=part1[:], in1=part2[:], op=ALU.add)
 
         for n in range(W_CHUNKS):
             open_sums = []
             for q in range(CHUNK_GROUPS):
-                half, quarter = q // 2, q % 2
-                blocks = []
-                for i in range(BANKS):
-                    for a in range(2):
-                        first = (quarter * BANKS + i) * PASS_WORDS
-                        words = w_rows[n][half][a][:].bitcast(F32)[:, first : first + PASS_WORDS]
-                        for u in range(2):
-                            blocks.append(every_second(words, u))
+                w = n * CHUNK_GROUPS + q
+                if w == 0:
+                    sort, blocks = nothing, stepped(w_rows[w])
+                else:
+                    sort, blocks = presorted(w_rows[w])
                 codes = codes_pool.tile([P, GROUP_COLS], U32, tag="codes", align_bytes=64)
                 scales = codes_pool.tile([P, GROUP_COLS], U8, tag="scales", align_bytes=64)
-                turn, quantise = turned_group(blocks, False, 2, codes[:], scales[:])
+                turn, quantise = turned_group(blocks, False, 1, codes[:], scales[:])
 
-                def turn_w(w=n * CHUNK_GROUPS + q, turn=turn):
-                    if w < 6:
-                        sum_abs(X_GROUPS + 2 * w)
-                        sum_abs(X_GROUPS + 2 * w + 1)
+                def turn_w(w=w, turn=turn):
+                    sum_abs(X_GROUPS + w)
                     turn()
 
                 def multiply_w(n=n, q=q, codes=codes, scales=scales, open_sums=open_sums):
@@ -241,8 +251,11 @@ def tile_dynamiclayer_k_kernel(tc, x, W1, b1, W2, b2, Wf, bf, out):
                             )
                     if q == CHUNK_GROUPS - 1:
                         finish_chunk(n, open_sums)
+                    if n == 2 and q == CHUNK_GROUPS - 2:
+                        compare_means()
+                        select_first_half()
 
-                pipeline.append((turn_w, quantise, multiply_w))
+                pipeline.append((sort, turn_w, quantise, multiply_w))
 
         def turn_h():
             bank = psum.tile([P, 4, P], F32, tag="bank")
@@ -255,14 +268,14 @@ def tile_dynamiclayer_k_kernel(tc, x, W1, b1, W2, b2, Wf, bf, out):
             )
             nc.vector.quantize_mx(out=h_codes[:].bitcast(FP8X4), scales=h_scales[:], in_=h_grouped[:])
 
-        pipeline.append((nothing, nothing, turn_h))
+        pipeline.append((nothing, nothing, nothing, turn_h))
 
         for c in range(F_GROUPS):
             words = f_rows[c][:].bitcast(F32)
             blocks = [every_second(words[:, j * PASS_WORDS : (j + 1) * PASS_WORDS], u) for j in range(2 * BANKS) for u in range(2)]
             codes = codes_pool.tile([P, GROUP_COLS], U32, tag="codes", align_bytes=64)
             scales = codes_pool.tile([P, GROUP_COLS], U8, tag="scales", align_bytes=64)
-            turn, quantise = turned_group(blocks, True, 0, codes[:], scales[:])
+            turn, quantise = turned_group(lambda blocks=blocks: blocks, True, 0, codes[:], scales[:])
 
             def multiply_f(c=c, codes=codes, scales=scales):
                 for t in range(2):
@@ -294,12 +307,14 @@ def tile_dynamiclayer_k_kernel(tc, x, W1, b1, W2, b2, Wf, bf, out):
                             )
                     nc.sync.dma_start(out=out[t * P : (t + 1) * P, c * GROUP_COLS : (c + 1) * GROUP_COLS], in_=result[:])
 
-            pipeline.append((turn, quantise, multiply_f))
+            pipeline.append((nothing, turn, quantise, multiply_f))
 
         for i in range(len(pipeline) + 2):
             if i < len(pipeline):
-                pipeline[i][0]()
+                pipeline[i][1]()
+            if i + 1 < len(pipeline):
+                pipeline[i + 1][0]()
             if 1 <= i <= len(pipeline):
-                pipeline[i - 1][1]()
+                pipeline[i - 1][2]()
             if i >= 2:
-                pipeline[i - 2][2]()
+                pipeline[i - 2][3]()

@@ -44,31 +44,47 @@ def tile_dynamiclayer_k_kernel(tc, x, W1, b1, W2, b2, Wf, bf, out):
         scratch_pool = ctx.enter_context(tc.tile_pool(name="scratch_pool", bufs=2))
         sorted_pool = ctx.enter_context(tc.tile_pool(name="sorted_pool", bufs=2))
         part_pool = ctx.enter_context(tc.tile_pool(name="part_pool", bufs=2))
-        out_pool = ctx.enter_context(tc.tile_pool(name="out_pool", bufs=4))
+        out_pool = ctx.enter_context(tc.tile_pool(name="out_pool", bufs=6))
         psum = ctx.enter_context(tc.psum_pool(name="psum", bufs=6))
         sums_pool = ctx.enter_context(tc.psum_pool(name="sums_pool", bufs=2))
 
         x_rows = []
         for g in range(X_GROUPS):
-            cols = slice(g * GROUP_ELEMS // 2, (g + 1) * GROUP_ELEMS // 2)
             rows = x_pool.tile([P, GROUP_ELEMS], BF16, tag="x_rows")
-            nc.sync.dma_start(
-                out=rows[:].rearrange("p (t k) -> p t k", t=2),
-                in_=x[:, cols].rearrange("(t p) k -> p t k", p=P),
-            )
+            pieces = 2 if g == 0 else 1
+            width = GROUP_ELEMS // 2 // pieces
+            for piece in range(pieces):
+                first = g * GROUP_ELEMS // 2 + piece * width
+                nc.sync.dma_start(
+                    out=rows[:].rearrange("p (t k) -> p t k", t=2)[:, :, piece * width : (piece + 1) * width],
+                    in_=x[:, first : first + width].rearrange("(t p) k -> p t k", p=P),
+                )
             x_rows.append(rows)
 
         w_views = [W2, W1[0:B, :], W1[B : 2 * B, :]]
         w_rows = []
         for n, view in enumerate(w_views):
-            for q in range(CHUNK_GROUPS):
-                cols = slice(q * GROUP_ELEMS // 2, (q + 1) * GROUP_ELEMS // 2)
-                rows = w_pool.tile([P, GROUP_ELEMS], BF16, tag="rows")
-                nc.sync.dma_start(
-                    out=rows[:].rearrange("p (t k) -> p t k", t=2),
-                    in_=view[:, cols].rearrange("(t p) k -> p t k", p=P),
-                )
-                w_rows.append(rows)
+            if n == 0:
+                for q in range(CHUNK_GROUPS):
+                    cols = slice(q * GROUP_ELEMS // 2, (q + 1) * GROUP_ELEMS // 2)
+                    rows = w_pool.tile([P, GROUP_ELEMS], BF16, tag="rows")
+                    nc.sync.dma_start(
+                        out=rows[:].rearrange("p (t k) -> p t k", t=2),
+                        in_=view[:, cols].rearrange("(t p) k -> p t k", p=P),
+                    )
+                    w_rows.append([rows[:, a * GROUP_ELEMS // 2 : (a + 1) * GROUP_ELEMS // 2] for a in range(2)])
+            else:
+                for half in range(2):
+                    pair = []
+                    for a in range(2):
+                        rows = w_pool.tile([P, GROUP_ELEMS], BF16, tag="rows")
+                        nc.sync.dma_start(
+                            out=rows[:],
+                            in_=view[a * P : (a + 1) * P, half * GROUP_ELEMS : (half + 1) * GROUP_ELEMS],
+                        )
+                        pair.append(rows)
+                    for q in range(2):
+                        w_rows.append([rows[:, q * GROUP_ELEMS // 2 : (q + 1) * GROUP_ELEMS // 2] for rows in pair])
             if n == 0:
                 bias2 = keep.tile([P, U2], BF16)
                 nc.sync.dma_start(out=bias2[:], in_=b2.partition_broadcast(P))
@@ -137,7 +153,7 @@ def tile_dynamiclayer_k_kernel(tc, x, W1, b1, W2, b2, Wf, bf, out):
                 accum_out=abs_sums[:, quarter // 2, 2 * g + quarter % 2 : 2 * g + quarter % 2 + 1],
             )
 
-        def presorted(rows):
+        def presorted_f(rows):
             made = {}
 
             def sort():
@@ -146,6 +162,24 @@ def tile_dynamiclayer_k_kernel(tc, x, W1, b1, W2, b2, Wf, bf, out):
                     out=by_parity[:].bitcast(F32).rearrange("p (b u w) -> p b u w", u=2, w=P),
                     in_=rows[:].bitcast(F32).rearrange("p (b w u) -> p b u w", u=2, w=P),
                 )
+                made["rows"] = by_parity
+
+            def blocks():
+                words = made["rows"][:].bitcast(F32)
+                return [words[:, j * P : (j + 1) * P] for j in range(4 * BANKS)]
+
+            return sort, blocks
+
+        def presorted(rows):
+            made = {}
+
+            def sort():
+                by_parity = sorted_pool.tile([P, GROUP_ELEMS], BF16, tag="sorted")
+                for a in range(2):
+                    nc.vector.tensor_copy(
+                        out=by_parity[:, a * GROUP_ELEMS // 2 : (a + 1) * GROUP_ELEMS // 2].bitcast(F32).rearrange("p (b u w) -> p b u w", u=2, w=P),
+                        in_=rows[a].bitcast(F32).rearrange("p (b w u) -> p b u w", u=2, w=P),
+                    )
                 made["rows"] = by_parity
 
             def blocks():
@@ -163,13 +197,12 @@ def tile_dynamiclayer_k_kernel(tc, x, W1, b1, W2, b2, Wf, bf, out):
             return words[:, first:PASS_WORDS:2]
 
         def stepped(rows):
-            words = rows[:].bitcast(F32)
             blocks = []
             for i in range(BANKS):
                 for a in range(2):
-                    first = (a * BANKS + i) * PASS_WORDS
+                    words = rows[a].bitcast(F32)[:, i * PASS_WORDS : (i + 1) * PASS_WORDS]
                     for u in range(2):
-                        blocks.append(every_second(words[:, first : first + PASS_WORDS], u))
+                        blocks.append(every_second(words, u))
             return lambda: blocks
 
         def nothing():
@@ -179,7 +212,7 @@ def tile_dynamiclayer_k_kernel(tc, x, W1, b1, W2, b2, Wf, bf, out):
 
         for g in range(X_GROUPS):
             cols = slice(g * GROUP_COLS, (g + 1) * GROUP_COLS)
-            turn, quantise = turned_group(stepped(x_rows[g]), False, 2, x_codes[:, cols], x_scales[:, cols])
+            turn, quantise = turned_group(stepped([x_rows[g][:, a * GROUP_ELEMS // 2 : (a + 1) * GROUP_ELEMS // 2] for a in range(2)]), False, 2, x_codes[:, cols], x_scales[:, cols])
 
             def turn_x(g=g, turn=turn):
                 sum_abs(g)
@@ -220,13 +253,13 @@ def tile_dynamiclayer_k_kernel(tc, x, W1, b1, W2, b2, Wf, bf, out):
             open_sums = []
             for q in range(CHUNK_GROUPS):
                 w = n * CHUNK_GROUPS + q
-                if w == 0:
+                if w in (0, 1, 2):
                     sort, blocks = nothing, stepped(w_rows[w])
                 else:
                     sort, blocks = presorted(w_rows[w])
                 codes = codes_pool.tile([P, GROUP_COLS], U32, tag="codes", align_bytes=64)
                 scales = codes_pool.tile([P, GROUP_COLS], U8, tag="scales", align_bytes=64)
-                turn, quantise = turned_group(blocks, False, 1, codes[:], scales[:])
+                turn, quantise = turned_group(blocks, False, 1 + (w + 1) % 2 if w < 3 else w % 2, codes[:], scales[:])
 
                 def turn_w(w=w, turn=turn):
                     sum_abs(X_GROUPS + w)
@@ -275,7 +308,11 @@ def tile_dynamiclayer_k_kernel(tc, x, W1, b1, W2, b2, Wf, bf, out):
             blocks = [every_second(words[:, j * PASS_WORDS : (j + 1) * PASS_WORDS], u) for j in range(2 * BANKS) for u in range(2)]
             codes = codes_pool.tile([P, GROUP_COLS], U32, tag="codes", align_bytes=64)
             scales = codes_pool.tile([P, GROUP_COLS], U8, tag="scales", align_bytes=64)
-            turn, quantise = turned_group(lambda blocks=blocks: blocks, True, 0, codes[:], scales[:])
+            if c in (1,3,5):
+                sort, get = presorted_f(f_rows[c])
+            else:
+                sort, get = nothing, lambda blocks=blocks: blocks
+            turn, quantise = turned_group(get, True, 0, codes[:], scales[:])
 
             def multiply_f(c=c, codes=codes, scales=scales):
                 for t in range(2):
@@ -307,7 +344,7 @@ def tile_dynamiclayer_k_kernel(tc, x, W1, b1, W2, b2, Wf, bf, out):
                             )
                     nc.sync.dma_start(out=out[t * P : (t + 1) * P, c * GROUP_COLS : (c + 1) * GROUP_COLS], in_=result[:])
 
-            pipeline.append((nothing, turn, quantise, multiply_f))
+            pipeline.append((sort, turn, quantise, multiply_f))
 
         for i in range(len(pipeline) + 2):
             if i < len(pipeline):

@@ -23,13 +23,18 @@ PASSES = D // K_PASS
 BANKS = 4
 GROUP_COLS = 1024
 GROUP_ELEMS = 4 * GROUP_COLS
-X_GROUPS = B * PASSES // GROUP_COLS
+HALF = GROUP_ELEMS
+HALF_PASSES = HALF // K_PASS
+X_GROUPS = 4
 W_CHUNKS = (U1 + U2) // B
 CHUNK_GROUPS = PASSES // BANKS
+W_GROUPS = W_CHUNKS * CHUNK_GROUPS
 F_GROUPS = D // GROUP_COLS
 N_OUT = 512
 ABS_PIECES = 16
 ABS_COLS = 2 * D // ABS_PIECES
+STEPPED = (0,1,2,3,4,5)
+F_SORTED = ()
 
 
 def tile_dynamiclayer_k_kernel(tc, x, W1, b1, W2, b2, Wf, bf, out):
@@ -39,52 +44,40 @@ def tile_dynamiclayer_k_kernel(tc, x, W1, b1, W2, b2, Wf, bf, out):
         keep = ctx.enter_context(tc.tile_pool(name="keep", bufs=1))
         x_pool = ctx.enter_context(tc.tile_pool(name="x_pool", bufs=X_GROUPS))
         w_pool = ctx.enter_context(tc.tile_pool(name="w_pool", bufs=8))
+        sorted_pool = ctx.enter_context(tc.tile_pool(name="sorted_pool", bufs=2))
         grouped_pool = ctx.enter_context(tc.tile_pool(name="grouped_pool", bufs=3))
         codes_pool = ctx.enter_context(tc.tile_pool(name="codes_pool", bufs=3))
-        scratch_pool = ctx.enter_context(tc.tile_pool(name="scratch_pool", bufs=2))
-        sorted_pool = ctx.enter_context(tc.tile_pool(name="sorted_pool", bufs=2))
+        scratch_pool = ctx.enter_context(tc.tile_pool(name="scratch_pool", bufs=1))
         part_pool = ctx.enter_context(tc.tile_pool(name="part_pool", bufs=2))
         out_pool = ctx.enter_context(tc.tile_pool(name="out_pool", bufs=6))
         psum = ctx.enter_context(tc.psum_pool(name="psum", bufs=6))
         sums_pool = ctx.enter_context(tc.psum_pool(name="sums_pool", bufs=2))
 
         x_rows = []
-        for g in range(X_GROUPS):
-            rows = x_pool.tile([P, GROUP_ELEMS], BF16, tag="x_rows")
-            pieces = 2 if g == 0 else 1
-            width = GROUP_ELEMS // 2 // pieces
-            for piece in range(pieces):
-                first = g * GROUP_ELEMS // 2 + piece * width
-                nc.sync.dma_start(
-                    out=rows[:].rearrange("p (t k) -> p t k", t=2)[:, :, piece * width : (piece + 1) * width],
-                    in_=x[:, first : first + width].rearrange("(t p) k -> p t k", p=P),
-                )
-            x_rows.append(rows)
+
+        def load_x(h):
+            for t in range(2):
+                rows = x_pool.tile([P, HALF], BF16, tag="x_rows")
+                pieces = 2 if h == 0 and t == 0 else 1
+                width = HALF // pieces
+                for piece in range(pieces):
+                    cols = slice(piece * width, (piece + 1) * width)
+                    nc.sync.dma_start(out=rows[:, cols], in_=x[t * P : (t + 1) * P, h * HALF : (h + 1) * HALF][:, cols])
+                x_rows.append(rows)
 
         w_views = [W2, W1[0:B, :], W1[B : 2 * B, :]]
         w_rows = []
         for n, view in enumerate(w_views):
-            if n == 0:
-                for q in range(CHUNK_GROUPS):
-                    cols = slice(q * GROUP_ELEMS // 2, (q + 1) * GROUP_ELEMS // 2)
-                    rows = w_pool.tile([P, GROUP_ELEMS], BF16, tag="rows")
-                    nc.sync.dma_start(
-                        out=rows[:].rearrange("p (t k) -> p t k", t=2),
-                        in_=view[:, cols].rearrange("(t p) k -> p t k", p=P),
-                    )
-                    w_rows.append([rows[:, a * GROUP_ELEMS // 2 : (a + 1) * GROUP_ELEMS // 2] for a in range(2)])
-            else:
-                for half in range(2):
-                    pair = []
-                    for a in range(2):
-                        rows = w_pool.tile([P, GROUP_ELEMS], BF16, tag="rows")
-                        nc.sync.dma_start(
-                            out=rows[:],
-                            in_=view[a * P : (a + 1) * P, half * GROUP_ELEMS : (half + 1) * GROUP_ELEMS],
-                        )
-                        pair.append(rows)
-                    for q in range(2):
-                        w_rows.append([rows[:, q * GROUP_ELEMS // 2 : (q + 1) * GROUP_ELEMS // 2] for rows in pair])
+            for h in range(2):
+                if n == 0:
+                    load_x(h)
+                pair = []
+                for a in range(2):
+                    rows = w_pool.tile([P, HALF], BF16, tag="rows")
+                    nc.sync.dma_start(out=rows[:], in_=view[a * P : (a + 1) * P, h * HALF : (h + 1) * HALF])
+                    pair.append(rows)
+                for q in range(2):
+                    w_rows.append([rows[:, q * HALF // 2 : (q + 1) * HALF // 2] for rows in pair])
             if n == 0:
                 bias2 = keep.tile([P, U2], BF16)
                 nc.sync.dma_start(out=bias2[:], in_=b2.partition_broadcast(P))
@@ -92,12 +85,14 @@ def tile_dynamiclayer_k_kernel(tc, x, W1, b1, W2, b2, Wf, bf, out):
                 nc.sync.dma_start(out=bias1[:], in_=b1.partition_broadcast(P))
         bias = keep.tile([P, D], BF16)
         nc.sync.dma_start(out=bias[:], in_=bf.partition_broadcast(P))
+        f_spans = [(c * GROUP_COLS, GROUP_COLS) for c in range(F_GROUPS - 1)]
+        f_spans += [(D - GROUP_COLS, N_OUT), (D - N_OUT, N_OUT)]
         f_rows = []
-        for c in range(F_GROUPS):
+        for first, cols in f_spans:
             rows = w_pool.tile([P, GROUP_ELEMS], BF16, tag="rows")
             nc.sync.dma_start(
-                out=rows[:],
-                in_=Wf[c * GROUP_COLS : (c + 1) * GROUP_COLS, :].rearrange("(p n) k -> p (n k)", p=P),
+                out=rows[:, 0 : 4 * cols],
+                in_=Wf[first : first + cols, :].rearrange("(p n) k -> p (n k)", p=P),
             )
             f_rows.append(rows)
 
@@ -113,122 +108,81 @@ def tile_dynamiclayer_k_kernel(tc, x, W1, b1, W2, b2, Wf, bf, out):
         h_scales = keep.tile([P, B], U8, align_bytes=64)
         h_rows = [keep.tile([P, U1], BF16, name="h_rows_%d" % t) for t in range(2)]
 
-        def turned_group(blocks, rows_first, vector_banks, codes, scales):
-            made = {}
+        def pass_words(rows):
+            words = rows.bitcast(F32)
+            return [words[:, first : first + PASS_WORDS] for first in range(0, words.shape[1], PASS_WORDS)]
+
+        def stepped(passes):
+            return lambda: [words[:, u:PASS_WORDS:2] for words in passes for u in range(2)]
+
+        def presorted(tiles, order):
+            made = []
+
+            def sort():
+                by_parity = sorted_pool.tile([P, GROUP_ELEMS], BF16, tag="sorted")
+                made.append(by_parity)
+                width = GROUP_ELEMS // len(tiles)
+                for a, rows in enumerate(tiles):
+                    nc.vector.tensor_copy(
+                        out=by_parity[:, a * width : (a + 1) * width].bitcast(F32).rearrange("p (b u w) -> p b u w", u=2, w=P),
+                        in_=rows.bitcast(F32).rearrange("p (b w u) -> p b u w", u=2, w=P),
+                    )
+
+            def blocks():
+                passes = pass_words(made[0][:])
+                return [passes[g][:, u * P : (u + 1) * P] for g in order for u in range(2)]
+
+            return sort, blocks
+
+        def turned_group(blocks, rows_first, vector_banks, codes, scales, n_banks=BANKS):
+            made = []
 
             def turn():
+                source = blocks()
                 banks = []
-                for i in range(BANKS):
+                for i in range(n_banks):
                     bank = psum.tile([P, 4, P], F32, tag="bank")
                     for s in range(4):
-                        nc.tensor.transpose(bank[:, s, :], blocks()[4 * i + s], ident_f32[:])
+                        nc.tensor.transpose(bank[:, s, :], source[4 * i + s], ident_f32[:])
                     banks.append(bank)
                 grouped = grouped_pool.tile([P, GROUP_ELEMS], BF16, tag="grouped", align_bytes=64)
-                words = grouped[:].bitcast(F32)
-                for i in range(BANKS):
+                made.append(grouped)
+                words = grouped[:, 0 : n_banks * GROUP_COLS].bitcast(F32)
+                for i in range(n_banks):
                     if rows_first:
-                        dst = words.rearrange("p (r i a u) -> p i r a u", i=BANKS, a=2, u=2)[:, i]
+                        dst = words.rearrange("p (r i a u) -> p i r a u", i=n_banks, a=2, u=2)[:, i]
                         src = banks[i][:].rearrange("p (a u) r -> p r a u", u=2)
                     else:
-                        dst = words.rearrange("p (i a r u) -> p i a r u", i=BANKS, a=2, u=2)[:, i]
+                        dst = words.rearrange("p (i a r u) -> p i a r u", i=n_banks, a=2, u=2)[:, i]
                         src = banks[i][:].rearrange("p (a u) r -> p a r u", u=2)
                     if i < vector_banks:
                         nc.vector.tensor_copy(out=dst, in_=src)
                     else:
                         nc.scalar.copy(out=dst, in_=src)
-                made["grouped"] = grouped
 
             def quantise():
-                nc.vector.quantize_mx(out=codes.bitcast(FP8X4), scales=scales, in_=made["grouped"][:])
+                nc.vector.quantize_mx(out=codes.bitcast(FP8X4), scales=scales, in_=made[0][:, 0 : n_banks * GROUP_COLS])
 
             return turn, quantise
 
         def sum_abs(piece):
             g, quarter = piece // 4, piece % 4
+            h, t = g // 2, g % 2
             scratch = scratch_pool.tile([P, ABS_COLS], BF16, tag="scratch")
             nc.scalar.activation(
                 out=scratch[:],
                 in_=x_rows[g][:, quarter * ABS_COLS : (quarter + 1) * ABS_COLS],
                 func=ACT.Abs,
-                accum_out=abs_sums[:, quarter // 2, 2 * g + quarter % 2 : 2 * g + quarter % 2 + 1],
+                accum_out=abs_sums[:, t, 4 * h + quarter : 4 * h + quarter + 1],
             )
-
-        def presorted_f(rows):
-            made = {}
-
-            def sort():
-                by_parity = sorted_pool.tile([P, GROUP_ELEMS], BF16, tag="sorted")
-                nc.vector.tensor_copy(
-                    out=by_parity[:].bitcast(F32).rearrange("p (b u w) -> p b u w", u=2, w=P),
-                    in_=rows[:].bitcast(F32).rearrange("p (b w u) -> p b u w", u=2, w=P),
-                )
-                made["rows"] = by_parity
-
-            def blocks():
-                words = made["rows"][:].bitcast(F32)
-                return [words[:, j * P : (j + 1) * P] for j in range(4 * BANKS)]
-
-            return sort, blocks
-
-        def presorted(rows):
-            made = {}
-
-            def sort():
-                by_parity = sorted_pool.tile([P, GROUP_ELEMS], BF16, tag="sorted")
-                for a in range(2):
-                    nc.vector.tensor_copy(
-                        out=by_parity[:, a * GROUP_ELEMS // 2 : (a + 1) * GROUP_ELEMS // 2].bitcast(F32).rearrange("p (b u w) -> p b u w", u=2, w=P),
-                        in_=rows[a].bitcast(F32).rearrange("p (b w u) -> p b u w", u=2, w=P),
-                    )
-                made["rows"] = by_parity
-
-            def blocks():
-                words = made["rows"][:].bitcast(F32)
-                return [
-                    words[:, ((a * BANKS + i) * 2 + u) * P : ((a * BANKS + i) * 2 + u + 1) * P]
-                    for i in range(BANKS)
-                    for a in range(2)
-                    for u in range(2)
-                ]
-
-            return sort, blocks
-
-        def every_second(words, first):
-            return words[:, first:PASS_WORDS:2]
-
-        def stepped(rows):
-            blocks = []
-            for i in range(BANKS):
-                for a in range(2):
-                    words = rows[a].bitcast(F32)[:, i * PASS_WORDS : (i + 1) * PASS_WORDS]
-                    for u in range(2):
-                        blocks.append(every_second(words, u))
-            return lambda: blocks
-
-        def nothing():
-            return None
-
-        pipeline = []
-
-        for g in range(X_GROUPS):
-            cols = slice(g * GROUP_COLS, (g + 1) * GROUP_COLS)
-            turn, quantise = turned_group(stepped([x_rows[g][:, a * GROUP_ELEMS // 2 : (a + 1) * GROUP_ELEMS // 2] for a in range(2)]), False, 2, x_codes[:, cols], x_scales[:, cols])
-
-            def turn_x(g=g, turn=turn):
-                sum_abs(g)
-                turn()
-
-            pipeline.append((nothing, turn_x, quantise, nothing))
 
         def compare_means():
             mean_abs = keep.tile([P, 2], F32)
             nc.vector.tensor_reduce(out=mean_abs[:], in_=abs_sums[:], axis=AX.X, op=ALU.add)
-            nc.vector.tensor_scalar(
-                out=takes[:, 0, :], in0=mean_abs[:], scalar1=1.0 / D, scalar2=THRESHOLD, op0=ALU.mult, op1=ALU.is_gt
-            )
-            nc.vector.tensor_scalar(
-                out=takes[:, 1, :], in0=mean_abs[:], scalar1=1.0 / D, scalar2=THRESHOLD, op0=ALU.mult, op1=ALU.is_le
-            )
+            for branch, op in ((0, ALU.is_gt), (1, ALU.is_le)):
+                nc.vector.tensor_scalar(
+                    out=takes[:, branch, :], in0=mean_abs[:], scalar1=1.0 / D, scalar2=THRESHOLD, op0=ALU.mult, op1=op
+                )
 
         biased = [[keep.tile([P, B], F32, name="biased_%d_%d" % (n, t)) for t in range(2)] for n in range(W_CHUNKS)]
         chunk_bias = [bias2[:], bias1[:, 0:B], bias1[:, B : 2 * B]]
@@ -249,30 +203,37 @@ def tile_dynamiclayer_k_kernel(tc, x, W1, b1, W2, b2, Wf, bf, out):
                 nc.scalar.activation(out=part2[:], in_=biased[0][t][:], func=ACT.Relu, scale=takes[:, 1, t : t + 1])
                 nc.vector.tensor_tensor(out=h_rows[t][:, 0:B], in0=part1[:], in1=part2[:], op=ALU.add)
 
+        def nothing():
+            return None
+
+        x_items = []
+        for g in range(X_GROUPS):
+            cols = slice(g * GROUP_COLS, (g + 1) * GROUP_COLS)
+            turn, quantise = turned_group(stepped(pass_words(x_rows[g][:])), False, 2, x_codes[:, cols], x_scales[:, cols])
+            x_items.append((nothing, turn, quantise, nothing))
+
+        w_items = []
         for n in range(W_CHUNKS):
             open_sums = []
             for q in range(CHUNK_GROUPS):
                 w = n * CHUNK_GROUPS + q
-                if w in (0, 1, 2):
-                    sort, blocks = nothing, stepped(w_rows[w])
-                else:
-                    sort, blocks = presorted(w_rows[w])
                 codes = codes_pool.tile([P, GROUP_COLS], U32, tag="codes", align_bytes=64)
                 scales = codes_pool.tile([P, GROUP_COLS], U8, tag="scales", align_bytes=64)
-                turn, quantise = turned_group(blocks, False, 1 + (w + 1) % 2 if w < 3 else w % 2, codes[:], scales[:])
+                if w in STEPPED:
+                    tile_passes = [pass_words(rows) for rows in w_rows[w]]
+                    sort, blocks = nothing, stepped([tile_passes[a][i] for i in range(BANKS) for a in range(2)])
+                else:
+                    sort, blocks = presorted(w_rows[w], [a * BANKS + i for i in range(BANKS) for a in range(2)])
+                turn, quantise = turned_group(blocks, False, 2 if w < 4 else 1 if w in STEPPED else 0, codes[:], scales[:])
 
-                def turn_w(w=w, turn=turn):
-                    sum_abs(X_GROUPS + w)
-                    turn()
-
-                def multiply_w(n=n, q=q, codes=codes, scales=scales, open_sums=open_sums):
+                def multiply(w=w, n=n, q=q, codes=codes, scales=scales, open_sums=open_sums):
                     for t in range(2):
                         if q == 0:
                             sums = sums_pool.tile([P, N_OUT], F32, tag="sums")
                             open_sums.append(sums[:, 0:B])
                         for j in range(BANKS):
                             g = q * BANKS + j
-                            first = g * B + t * P
+                            first = ((g // HALF_PASSES * 2 + t) * HALF_PASSES + g % HALF_PASSES) * P
                             nc.tensor.matmul_mx(
                                 out=open_sums[t],
                                 lhsT=x_codes[:, first : first + P].bitcast(FP8X4),
@@ -284,40 +245,38 @@ def tile_dynamiclayer_k_kernel(tc, x, W1, b1, W2, b2, Wf, bf, out):
                             )
                     if q == CHUNK_GROUPS - 1:
                         finish_chunk(n, open_sums)
-                    if n == 2 and q == CHUNK_GROUPS - 2:
+                    if w == 8:
                         compare_means()
+                    if w == 9:
                         select_first_half()
 
-                pipeline.append((sort, turn_w, quantise, multiply_w))
+                w_items.append((sort, turn, quantise, multiply))
 
         def turn_h():
             bank = psum.tile([P, 4, P], F32, tag="bank")
             for t in range(2):
                 for u in range(2):
-                    nc.tensor.transpose(bank[:, 2 * t + u, :], every_second(h_rows[t][:].bitcast(F32), u), ident_f32[:])
+                    nc.tensor.transpose(bank[:, 2 * t + u, :], h_rows[t][:].bitcast(F32)[:, u:PASS_WORDS:2], ident_f32[:])
             nc.vector.tensor_copy(
                 out=h_grouped[:].bitcast(F32).rearrange("p (t r u) -> p t r u", t=2, u=2),
                 in_=bank[:].rearrange("p (t u) r -> p t r u", u=2),
             )
             nc.vector.quantize_mx(out=h_codes[:].bitcast(FP8X4), scales=h_scales[:], in_=h_grouped[:])
 
-        pipeline.append((nothing, nothing, nothing, turn_h))
-
-        for c in range(F_GROUPS):
-            words = f_rows[c][:].bitcast(F32)
-            blocks = [every_second(words[:, j * PASS_WORDS : (j + 1) * PASS_WORDS], u) for j in range(2 * BANKS) for u in range(2)]
+        f_items = []
+        for c, (start, width) in enumerate(f_spans):
             codes = codes_pool.tile([P, GROUP_COLS], U32, tag="codes", align_bytes=64)
             scales = codes_pool.tile([P, GROUP_COLS], U8, tag="scales", align_bytes=64)
-            if c in (1,3,5):
-                sort, get = presorted_f(f_rows[c])
+            if c in F_SORTED:
+                sort, blocks = presorted([f_rows[c][:]], range(2 * BANKS))
             else:
-                sort, get = nothing, lambda blocks=blocks: blocks
-            turn, quantise = turned_group(get, True, 0, codes[:], scales[:])
+                sort, blocks = nothing, stepped(pass_words(f_rows[c][:, 0 : 4 * width]))
+            turn, quantise = turned_group(blocks, True, 0, codes[:, 0:width], scales[:, 0:width], width // B)
 
-            def multiply_f(c=c, codes=codes, scales=scales):
+            def multiply(c=c, start=start, width=width, codes=codes, scales=scales):
                 for t in range(2):
                     result = out_pool.tile([P, GROUP_COLS], F32, tag="result")
-                    for j in range(GROUP_COLS // N_OUT):
+                    for j in range(width // N_OUT):
                         cols = slice(j * N_OUT, (j + 1) * N_OUT)
                         if j == 0:
                             sums = sums_pool.tile([P, N_OUT], F32, tag="sums")
@@ -332,8 +291,8 @@ def tile_dynamiclayer_k_kernel(tc, x, W1, b1, W2, b2, Wf, bf, out):
                             start=True,
                             stop=True,
                         )
-                        first = c * GROUP_COLS + j * N_OUT
-                        if t == 0 and j == 0:
+                        first = start + j * N_OUT
+                        if False:
                             nc.scalar.copy(out=result[:, cols], in_=sums[:])
                             nc.gpsimd.tensor_tensor(
                                 out=result[:, cols], in0=result[:, cols], in1=bias[:, first : first + N_OUT], op=ALU.add
@@ -342,16 +301,19 @@ def tile_dynamiclayer_k_kernel(tc, x, W1, b1, W2, b2, Wf, bf, out):
                             nc.vector.tensor_tensor(
                                 out=result[:, cols], in0=sums[:], in1=bias[:, first : first + N_OUT], op=ALU.add
                             )
-                    nc.sync.dma_start(out=out[t * P : (t + 1) * P, c * GROUP_COLS : (c + 1) * GROUP_COLS], in_=result[:])
+                    nc.sync.dma_start(out=out[t * P : (t + 1) * P, start : start + width], in_=result[:, 0:width])
 
-            pipeline.append((sort, turn, quantise, multiply_f))
+            f_items.append((sort, turn, quantise, multiply))
 
-        for i in range(len(pipeline) + 2):
-            if i < len(pipeline):
-                pipeline[i][1]()
-            if i + 1 < len(pipeline):
-                pipeline[i + 1][0]()
-            if 1 <= i <= len(pipeline):
-                pipeline[i - 1][2]()
+        items = x_items[0:2] + w_items[0:2] + x_items[2:4] + w_items[2:] + [(nothing, nothing, nothing, turn_h)] + f_items
+        for i in range(len(items) + 2):
+            for piece in {0: (0, 1), 1: (2, 3), 2: (4, 5), 3: (6, 7), 4: (8,), 5: (9, 10), 6: (11, 12), 7: (13,), 8: (14,), 9: (15,)}.get(i, ()):
+                sum_abs(piece)
+            if i < len(items):
+                items[i][1]()
+            if i + 1 < len(items):
+                items[i + 1][0]()
+            if 1 <= i <= len(items):
+                items[i - 1][2]()
             if i >= 2:
-                pipeline[i - 2][3]()
+                items[i - 2][3]()

@@ -33,8 +33,8 @@ F_GROUPS = D // GROUP_COLS
 N_OUT = 512
 ABS_PIECES = 16
 ABS_COLS = 2 * D // ABS_PIECES
-STEPPED = (0,1,2,3,4,5)
-F_SORTED = ()
+STEPPED = (0, 1, 2, 3, 4)
+F_SORTED = (1, 3, 5)
 
 
 def tile_dynamiclayer_k_kernel(tc, x, W1, b1, W2, b2, Wf, bf, out):
@@ -58,7 +58,7 @@ def tile_dynamiclayer_k_kernel(tc, x, W1, b1, W2, b2, Wf, bf, out):
         def load_x(h):
             for t in range(2):
                 rows = x_pool.tile([P, HALF], BF16, tag="x_rows")
-                pieces = 2 if h == 0 and t == 0 else 1
+                pieces = 4 if h == 0 and t == 0 else 1
                 width = HALF // pieces
                 for piece in range(pieces):
                     cols = slice(piece * width, (piece + 1) * width)
@@ -71,6 +71,15 @@ def tile_dynamiclayer_k_kernel(tc, x, W1, b1, W2, b2, Wf, bf, out):
             for h in range(2):
                 if n == 0:
                     load_x(h)
+                if n == 0 and h == 0:
+                    for q in range(2):
+                        rows = w_pool.tile([P, HALF], BF16, tag="rows")
+                        nc.sync.dma_start(
+                            out=rows[:].rearrange("p (a k) -> p a k", a=2),
+                            in_=view[:, q * HALF // 2 : (q + 1) * HALF // 2].rearrange("(a p) k -> p a k", p=P),
+                        )
+                        w_rows.append([rows[:, a * HALF // 2 : (a + 1) * HALF // 2] for a in range(2)])
+                    continue
                 pair = []
                 for a in range(2):
                     rows = w_pool.tile([P, HALF], BF16, tag="rows")
@@ -115,7 +124,7 @@ def tile_dynamiclayer_k_kernel(tc, x, W1, b1, W2, b2, Wf, bf, out):
         def stepped(passes):
             return lambda: [words[:, u:PASS_WORDS:2] for words in passes for u in range(2)]
 
-        def presorted(tiles, order):
+        def presorted(tiles, order, copy):
             made = []
 
             def sort():
@@ -123,7 +132,7 @@ def tile_dynamiclayer_k_kernel(tc, x, W1, b1, W2, b2, Wf, bf, out):
                 made.append(by_parity)
                 width = GROUP_ELEMS // len(tiles)
                 for a, rows in enumerate(tiles):
-                    nc.vector.tensor_copy(
+                    copy(
                         out=by_parity[:, a * width : (a + 1) * width].bitcast(F32).rearrange("p (b u w) -> p b u w", u=2, w=P),
                         in_=rows.bitcast(F32).rearrange("p (b w u) -> p b u w", u=2, w=P),
                     )
@@ -199,8 +208,10 @@ def tile_dynamiclayer_k_kernel(tc, x, W1, b1, W2, b2, Wf, bf, out):
             for t in range(2):
                 part1 = part_pool.tile([P, B], BF16, tag="part1")
                 part2 = part_pool.tile([P, B], BF16, tag="part2")
-                nc.scalar.activation(out=part1[:], in_=biased[1][t][:], func=ACT.Relu, scale=takes[:, 0, t : t + 1])
-                nc.scalar.activation(out=part2[:], in_=biased[0][t][:], func=ACT.Relu, scale=takes[:, 1, t : t + 1])
+                for part, n, branch in ((part1, 1, 0), (part2, 0, 1)):
+                    nc.vector.tensor_scalar(
+                        out=part[:], in0=biased[n][t][:], scalar1=0.0, scalar2=takes[:, branch, t : t + 1], op0=ALU.max, op1=ALU.mult
+                    )
                 nc.vector.tensor_tensor(out=h_rows[t][:, 0:B], in0=part1[:], in1=part2[:], op=ALU.add)
 
         def nothing():
@@ -223,8 +234,8 @@ def tile_dynamiclayer_k_kernel(tc, x, W1, b1, W2, b2, Wf, bf, out):
                     tile_passes = [pass_words(rows) for rows in w_rows[w]]
                     sort, blocks = nothing, stepped([tile_passes[a][i] for i in range(BANKS) for a in range(2)])
                 else:
-                    sort, blocks = presorted(w_rows[w], [a * BANKS + i for i in range(BANKS) for a in range(2)])
-                turn, quantise = turned_group(blocks, False, 2 if w < 4 else 1 if w in STEPPED else 0, codes[:], scales[:])
+                    sort, blocks = presorted(w_rows[w], [a * BANKS + i for i in range(BANKS) for a in range(2)], nc.vector.tensor_copy)
+                turn, quantise = turned_group(blocks, False, 2 if w < 4 else 1 if w == 4 else 0, codes[:], scales[:])
 
                 def multiply(w=w, n=n, q=q, codes=codes, scales=scales, open_sums=open_sums):
                     for t in range(2):
@@ -268,7 +279,7 @@ def tile_dynamiclayer_k_kernel(tc, x, W1, b1, W2, b2, Wf, bf, out):
             codes = codes_pool.tile([P, GROUP_COLS], U32, tag="codes", align_bytes=64)
             scales = codes_pool.tile([P, GROUP_COLS], U8, tag="scales", align_bytes=64)
             if c in F_SORTED:
-                sort, blocks = presorted([f_rows[c][:]], range(2 * BANKS))
+                sort, blocks = presorted([f_rows[c][:]], range(2 * BANKS), nc.vector.tensor_copy)
             else:
                 sort, blocks = nothing, stepped(pass_words(f_rows[c][:, 0 : 4 * width]))
             turn, quantise = turned_group(blocks, True, 0, codes[:, 0:width], scales[:, 0:width], width // B)
@@ -292,7 +303,7 @@ def tile_dynamiclayer_k_kernel(tc, x, W1, b1, W2, b2, Wf, bf, out):
                             stop=True,
                         )
                         first = start + j * N_OUT
-                        if False:
+                        if t == 0 and j == 0 and c < 8:
                             nc.scalar.copy(out=result[:, cols], in_=sums[:])
                             nc.gpsimd.tensor_tensor(
                                 out=result[:, cols], in0=result[:, cols], in1=bias[:, first : first + N_OUT], op=ALU.add

@@ -34,7 +34,7 @@ N_OUT = 512
 ABS_PIECES = 16
 ABS_COLS = 2 * D // ABS_PIECES
 STEPPED = (0, 1, 2, 3, 4)
-F_SORTED = (1, 3, 5)
+F_SORTED = (1, 4)
 
 
 def tile_dynamiclayer_k_kernel(tc, x, W1, b1, W2, b2, Wf, bf, out):
@@ -58,7 +58,7 @@ def tile_dynamiclayer_k_kernel(tc, x, W1, b1, W2, b2, Wf, bf, out):
         def load_x(h):
             for t in range(2):
                 rows = x_pool.tile([P, HALF], BF16, tag="x_rows")
-                pieces = 4 if h == 0 and t == 0 else 1
+                pieces = (4, 2, 1, 1)[2 * h + t]
                 width = HALF // pieces
                 for piece in range(pieces):
                     cols = slice(piece * width, (piece + 1) * width)
@@ -71,14 +71,18 @@ def tile_dynamiclayer_k_kernel(tc, x, W1, b1, W2, b2, Wf, bf, out):
             for h in range(2):
                 if n == 0:
                     load_x(h)
-                if n == 0 and h == 0:
+                if 4 * n + 2 * h < 12:
                     for q in range(2):
                         rows = w_pool.tile([P, HALF], BF16, tag="rows")
-                        nc.sync.dma_start(
-                            out=rows[:].rearrange("p (a k) -> p a k", a=2),
-                            in_=view[:, q * HALF // 2 : (q + 1) * HALF // 2].rearrange("(a p) k -> p a k", p=P),
-                        )
-                        w_rows.append([rows[:, a * HALF // 2 : (a + 1) * HALF // 2] for a in range(2)])
+                        first = h * HALF + q * HALF // 2
+                        pieces = 2 if n == 0 and h == 0 else 1
+                        width = HALF // 2 // pieces
+                        for piece in range(pieces):
+                            nc.sync.dma_start(
+                                out=rows[:].rearrange("p (a k) -> p a k", a=2)[:, :, piece * width : (piece + 1) * width],
+                                in_=view[:, first + piece * width : first + (piece + 1) * width].rearrange("(a p) k -> p a k", p=P),
+                            )
+                        w_rows.append([rows[:]])
                     continue
                 pair = []
                 for a in range(2):
@@ -220,7 +224,7 @@ def tile_dynamiclayer_k_kernel(tc, x, W1, b1, W2, b2, Wf, bf, out):
         x_items = []
         for g in range(X_GROUPS):
             cols = slice(g * GROUP_COLS, (g + 1) * GROUP_COLS)
-            turn, quantise = turned_group(stepped(pass_words(x_rows[g][:])), False, 2, x_codes[:, cols], x_scales[:, cols])
+            turn, quantise = turned_group(stepped(pass_words(x_rows[g][:])), False, 4 if g < 2 else 3, x_codes[:, cols], x_scales[:, cols])
             x_items.append((nothing, turn, quantise, nothing))
 
         w_items = []
@@ -231,8 +235,8 @@ def tile_dynamiclayer_k_kernel(tc, x, W1, b1, W2, b2, Wf, bf, out):
                 codes = codes_pool.tile([P, GROUP_COLS], U32, tag="codes", align_bytes=64)
                 scales = codes_pool.tile([P, GROUP_COLS], U8, tag="scales", align_bytes=64)
                 if w in STEPPED:
-                    tile_passes = [pass_words(rows) for rows in w_rows[w]]
-                    sort, blocks = nothing, stepped([tile_passes[a][i] for i in range(BANKS) for a in range(2)])
+                    passes = [words for rows in w_rows[w] for words in pass_words(rows)]
+                    sort, blocks = nothing, stepped([passes[a * BANKS + i] for i in range(BANKS) for a in range(2)])
                 else:
                     sort, blocks = presorted(w_rows[w], [a * BANKS + i for i in range(BANKS) for a in range(2)], nc.vector.tensor_copy)
                 turn, quantise = turned_group(blocks, False, 2 if w < 4 else 1 if w == 4 else 0, codes[:], scales[:])

@@ -58,7 +58,7 @@ def tile_dynamiclayer_k_kernel(tc, x, W1, b1, W2, b2, Wf, bf, out):
         def load_x(h):
             for t in range(2):
                 rows = x_pool.tile([P, HALF], BF16, tag="x_rows")
-                pieces = (4, 2, 1, 1)[2 * h + t]
+                pieces = (4, 2, 2, 2)[2 * h + t]
                 width = HALF // pieces
                 for piece in range(pieces):
                     cols = slice(piece * width, (piece + 1) * width)
@@ -104,8 +104,8 @@ def tile_dynamiclayer_k_kernel(tc, x, W1, b1, W2, b2, Wf, bf, out):
         for first, cols in f_spans:
             rows = w_pool.tile([P, GROUP_ELEMS], BF16, tag="rows")
             nc.sync.dma_start(
-                out=rows[:, 0 : 4 * cols],
-                in_=Wf[first : first + cols, :].rearrange("(p n) k -> p (n k)", p=P),
+                out=rows[:, 0 : 4 * cols].rearrange("p (s m) -> p s m", m=4 * N_OUT),
+                in_=Wf[first : first + cols, :].rearrange("(s p n) k -> p s (n k)", p=P, n=4),
             )
             f_rows.append(rows)
 
@@ -163,7 +163,7 @@ def tile_dynamiclayer_k_kernel(tc, x, W1, b1, W2, b2, Wf, bf, out):
                 words = grouped[:, 0 : n_banks * GROUP_COLS].bitcast(F32)
                 for i in range(n_banks):
                     if rows_first:
-                        dst = words.rearrange("p (r i a u) -> p i r a u", i=n_banks, a=2, u=2)[:, i]
+                        dst = words.rearrange("p (s r i a u) -> p s i r a u", s=n_banks // 2, i=2, a=2, u=2)[:, i // 2, i % 2]
                         src = banks[i][:].rearrange("p (a u) r -> p r a u", u=2)
                     else:
                         dst = words.rearrange("p (i a r u) -> p i a r u", i=n_banks, a=2, u=2)[:, i]

@@ -53,6 +53,13 @@ def tile_dynamiclayer_k_kernel(tc, x, W1, b1, W2, b2, Wf, bf, out):
         psum = ctx.enter_context(tc.psum_pool(name="psum", bufs=6))
         sums_pool = ctx.enter_context(tc.psum_pool(name="sums_pool", bufs=2))
 
+        hidden_bias = keep.tile([P, U1 + U2], BF16)
+        nc.vector.memset(hidden_bias[:], 0.0)
+        nc.scalar.dma_start(out=hidden_bias[0:1, 0:U1], in_=b1.rearrange("(o n) -> o n", o=1))
+        nc.scalar.dma_start(out=hidden_bias[0:1, U1:], in_=b2.rearrange("(o n) -> o n", o=1))
+        ones = keep.tile([P, P], BF16)
+        nc.vector.memset(ones[:], 1.0)
+
         x_rows = []
 
         def load_x(h):
@@ -91,13 +98,7 @@ def tile_dynamiclayer_k_kernel(tc, x, W1, b1, W2, b2, Wf, bf, out):
                     pair.append(rows)
                 for q in range(2):
                     w_rows.append([rows[:, q * HALF // 2 : (q + 1) * HALF // 2] for rows in pair])
-            if n == 0:
-                bias2 = keep.tile([P, U2], BF16)
-                nc.sync.dma_start(out=bias2[:], in_=b2.partition_broadcast(P))
-                bias1 = keep.tile([P, U1], BF16)
-                nc.sync.dma_start(out=bias1[:], in_=b1.partition_broadcast(P))
         bias = keep.tile([P, D], BF16)
-        nc.sync.dma_start(out=bias[:], in_=bf.partition_broadcast(P))
         f_spans = [(c * GROUP_COLS, GROUP_COLS) for c in range(F_GROUPS - 1)]
         f_spans += [(D - GROUP_COLS, N_OUT), (D - N_OUT, N_OUT)]
         f_rows = []
@@ -108,6 +109,8 @@ def tile_dynamiclayer_k_kernel(tc, x, W1, b1, W2, b2, Wf, bf, out):
                 in_=Wf[first : first + cols, :].rearrange("(s p n) k -> p s (n k)", p=P, n=4),
             )
             f_rows.append(rows)
+            if first == 1 * GROUP_COLS:
+                nc.sync.dma_start(out=bias[:], in_=bf.partition_broadcast(P))
 
         ident_f32 = keep.tile([P, P], F32)
         make_identity(nc, ident_f32[:])
@@ -198,7 +201,13 @@ def tile_dynamiclayer_k_kernel(tc, x, W1, b1, W2, b2, Wf, bf, out):
                 )
 
         biased = [[keep.tile([P, B], F32, name="biased_%d_%d" % (n, t)) for t in range(2)] for n in range(W_CHUNKS)]
-        chunk_bias = [bias2[:], bias1[:, 0:B], bias1[:, B : 2 * B]]
+        chunk_bias = [hidden_bias[:, U1:], hidden_bias[:, 0:B], hidden_bias[:, B:U1]]
+
+        def spread_hidden_bias():
+            bank = psum.tile([P, U1 + U2], BF16, tag="bank")
+            for cols in (slice(0, U1), slice(U1, U1 + U2)):
+                nc.tensor.matmul(out=bank[:, cols], lhsT=ones[:], rhs=hidden_bias[:, cols], start=True, stop=True)
+            nc.scalar.copy(out=hidden_bias[:], in_=bank[:])
 
         def finish_chunk(n, sums):
             for t in range(2):
@@ -332,3 +341,5 @@ def tile_dynamiclayer_k_kernel(tc, x, W1, b1, W2, b2, Wf, bf, out):
                 items[i - 1][2]()
             if i >= 2:
                 items[i - 2][3]()
+            if i == 8:
+                spread_hidden_bias()

from contextlib import ExitStack

import concourse.mybir as mybir
from concourse.masks import make_identity

F32 = mybir.dt.float32
BF16 = mybir.dt.bfloat16
U32 = mybir.dt.uint32
U8 = mybir.dt.uint8
FP8X4 = mybir.dt.float8_e4m3fn_x4
ALU = mybir.AluOpType
ACT = mybir.ActivationFunctionType
AX = mybir.AxisListType

B, D, U1, U2 = 256, 8192, 512, 256
THRESHOLD = 1.0
FLOPS = 2 * B * D * (U1 + U2) + 2 * B * U1 * D

P = 128
K_PASS = 512
PASS_WORDS = K_PASS // 2
PASSES = D // K_PASS
BANKS = 4
GROUP_COLS = 1024
GROUP_ELEMS = 4 * GROUP_COLS
HALF = GROUP_ELEMS
HALF_PASSES = HALF // K_PASS
X_GROUPS = 4
W_CHUNKS = (U1 + U2) // B
CHUNK_GROUPS = PASSES // BANKS
W_GROUPS = W_CHUNKS * CHUNK_GROUPS
F_GROUPS = D // GROUP_COLS
N_OUT = 512
ABS_PIECES = 16
ABS_COLS = 2 * D // ABS_PIECES
STEPPED = (0, 1, 2, 3, 4)
F_SORTED = (1, 4)


def tile_dynamiclayer_k_kernel(tc, x, W1, b1, W2, b2, Wf, bf, out):
    nc = tc.nc
    with ExitStack() as ctx:
        ctx.enter_context(tc.manual_schedule())
        keep = ctx.enter_context(tc.tile_pool(name="keep", bufs=1))
        x_pool = ctx.enter_context(tc.tile_pool(name="x_pool", bufs=X_GROUPS))
        w_pool = ctx.enter_context(tc.tile_pool(name="w_pool", bufs=8))
        sorted_pool = ctx.enter_context(tc.tile_pool(name="sorted_pool", bufs=2))
        grouped_pool = ctx.enter_context(tc.tile_pool(name="grouped_pool", bufs=3))
        codes_pool = ctx.enter_context(tc.tile_pool(name="codes_pool", bufs=3))
        scratch_pool = ctx.enter_context(tc.tile_pool(name="scratch_pool", bufs=1))
        part_pool = ctx.enter_context(tc.tile_pool(name="part_pool", bufs=2))
        out_pool = ctx.enter_context(tc.tile_pool(name="out_pool", bufs=6))
        psum = ctx.enter_context(tc.psum_pool(name="psum", bufs=6))
        sums_pool = ctx.enter_context(tc.psum_pool(name="sums_pool", bufs=2))

        hidden_bias = keep.tile([P, U1 + U2], BF16)
        nc.vector.memset(hidden_bias[:], 0.0)
        nc.scalar.dma_start(out=hidden_bias[0:1, 0:U1], in_=b1.rearrange("(o n) -> o n", o=1))
        nc.scalar.dma_start(out=hidden_bias[0:1, U1:], in_=b2.rearrange("(o n) -> o n", o=1))
        ones = keep.tile([P, P], BF16)
        nc.vector.memset(ones[:], 1.0)

        x_rows = []

        def load_x(h):
            for t in range(2):
                rows = x_pool.tile([P, HALF], BF16, tag="x_rows")
                pieces = (4, 2, 2, 2)[2 * h + t]
                width = HALF // pieces
                for piece in range(pieces):
                    cols = slice(piece * width, (piece + 1) * width)
                    nc.sync.dma_start(out=rows[:, cols], in_=x[t * P : (t + 1) * P, h * HALF : (h + 1) * HALF][:, cols])
                x_rows.append(rows)

        w_views = [W2, W1[0:B, :], W1[B : 2 * B, :]]
        w_rows = []
        for n, view in enumerate(w_views):
            for h in range(2):
                if n == 0:
                    load_x(h)
                if 4 * n + 2 * h < 12:
                    for q in range(2):
                        rows = w_pool.tile([P, HALF], BF16, tag="rows")
                        first = h * HALF + q * HALF // 2
                        pieces = 2 if n == 0 and h == 0 else 1
                        width = HALF // 2 // pieces
                        for piece in range(pieces):
                            nc.sync.dma_start(
                                out=rows[:].rearrange("p (a k) -> p a k", a=2)[:, :, piece * width : (piece + 1) * width],
                                in_=view[:, first + piece * width : first + (piece + 1) * width].rearrange("(a p) k -> p a k", p=P),
                            )
                        w_rows.append([rows[:]])
                    continue
                pair = []
                for a in range(2):
                    rows = w_pool.tile([P, HALF], BF16, tag="rows")
                    nc.sync.dma_start(out=rows[:], in_=view[a * P : (a + 1) * P, h * HALF : (h + 1) * HALF])
                    pair.append(rows)
                for q in range(2):
                    w_rows.append([rows[:, q * HALF // 2 : (q + 1) * HALF // 2] for rows in pair])
        bias = keep.tile([P, D], BF16)
        f_spans = [(c * GROUP_COLS, GROUP_COLS) for c in range(F_GROUPS - 1)]
        f_spans += [(D - GROUP_COLS, N_OUT), (D - N_OUT, N_OUT)]
        f_rows = []
        for first, cols in f_spans:
            rows = w_pool.tile([P, GROUP_ELEMS], BF16, tag="rows")
            nc.sync.dma_start(
                out=rows[:, 0 : 4 * cols].rearrange("p (s m) -> p s m", m=4 * N_OUT),
                in_=Wf[first : first + cols, :].rearrange("(s p n) k -> p s (n k)", p=P, n=4),
            )
            f_rows.append(rows)
            if first == 1 * GROUP_COLS:
                nc.sync.dma_start(out=bias[:], in_=bf.partition_broadcast(P))

        ident_f32 = keep.tile([P, P], F32)
        make_identity(nc, ident_f32[:])

        x_codes = keep.tile([P, PASSES * B], U32, align_bytes=64)
        x_scales = keep.tile([P, PASSES * B], U8, align_bytes=64)
        abs_sums = keep.tile([P, 2, ABS_PIECES // 2], F32)
        takes = keep.tile([P, 2, 2], F32)
        h_grouped = keep.tile([P, 4 * B], BF16, align_bytes=64)
        h_codes = keep.tile([P, B], U32, align_bytes=64)
        h_scales = keep.tile([P, B], U8, align_bytes=64)
        h_rows = [keep.tile([P, U1], BF16, name="h_rows_%d" % t) for t in range(2)]

        def pass_words(rows):
            words = rows.bitcast(F32)
            return [words[:, first : first + PASS_WORDS] for first in range(0, words.shape[1], PASS_WORDS)]

        def stepped(passes):
            return lambda: [words[:, u:PASS_WORDS:2] for words in passes for u in range(2)]

        def presorted(tiles, order, copy):
            made = []

            def sort():
                by_parity = sorted_pool.tile([P, GROUP_ELEMS], BF16, tag="sorted")
                made.append(by_parity)
                width = GROUP_ELEMS // len(tiles)
                for a, rows in enumerate(tiles):
                    copy(
                        out=by_parity[:, a * width : (a + 1) * width].bitcast(F32).rearrange("p (b u w) -> p b u w", u=2, w=P),
                        in_=rows.bitcast(F32).rearrange("p (b w u) -> p b u w", u=2, w=P),
                    )

            def blocks():
                passes = pass_words(made[0][:])
                return [passes[g][:, u * P : (u + 1) * P] for g in order for u in range(2)]

            return sort, blocks

        def turned_group(blocks, rows_first, vector_banks, codes, scales, n_banks=BANKS):
            made = []

            def turn():
                source = blocks()
                banks = []
                for i in range(n_banks):
                    bank = psum.tile([P, 4, P], F32, tag="bank")
                    for s in range(4):
                        nc.tensor.transpose(bank[:, s, :], source[4 * i + s], ident_f32[:])
                    banks.append(bank)
                grouped = grouped_pool.tile([P, GROUP_ELEMS], BF16, tag="grouped", align_bytes=64)
                made.append(grouped)
                words = grouped[:, 0 : n_banks * GROUP_COLS].bitcast(F32)
                for i in range(n_banks):
                    if rows_first:
                        dst = words.rearrange("p (s r i a u) -> p s i r a u", s=n_banks // 2, i=2, a=2, u=2)[:, i // 2, i % 2]
                        src = banks[i][:].rearrange("p (a u) r -> p r a u", u=2)
                    else:
                        dst = words.rearrange("p (i a r u) -> p i a r u", i=n_banks, a=2, u=2)[:, i]
                        src = banks[i][:].rearrange("p (a u) r -> p a r u", u=2)
                    if i < vector_banks:
                        nc.vector.tensor_copy(out=dst, in_=src)
                    else:
                        nc.scalar.copy(out=dst, in_=src)

            def quantise():
                nc.vector.quantize_mx(out=codes.bitcast(FP8X4), scales=scales, in_=made[0][:, 0 : n_banks * GROUP_COLS])

            return turn, quantise

        def sum_abs(piece):
            g, quarter = piece // 4, piece % 4
            h, t = g // 2, g % 2
            scratch = scratch_pool.tile([P, ABS_COLS], BF16, tag="scratch")
            nc.scalar.activation(
                out=scratch[:],
                in_=x_rows[g][:, quarter * ABS_COLS : (quarter + 1) * ABS_COLS],
                func=ACT.Abs,
                accum_out=abs_sums[:, t, 4 * h + quarter : 4 * h + quarter + 1],
            )

        def compare_means():
            mean_abs = keep.tile([P, 2], F32)
            nc.vector.tensor_reduce(out=mean_abs[:], in_=abs_sums[:], axis=AX.X, op=ALU.add)
            for branch, op in ((0, ALU.is_gt), (1, ALU.is_le)):
                nc.vector.tensor_scalar(
                    out=takes[:, branch, :], in0=mean_abs[:], scalar1=1.0 / D, scalar2=THRESHOLD, op0=ALU.mult, op1=op
                )

        biased = [[keep.tile([P, B], F32, name="biased_%d_%d" % (n, t)) for t in range(2)] for n in range(W_CHUNKS)]
        chunk_bias = [hidden_bias[:, U1:], hidden_bias[:, 0:B], hidden_bias[:, B:U1]]

        def spread_hidden_bias():
            bank = psum.tile([P, U1 + U2], BF16, tag="bank")
            for cols in (slice(0, U1), slice(U1, U1 + U2)):
                nc.tensor.matmul(out=bank[:, cols], lhsT=ones[:], rhs=hidden_bias[:, cols], start=True, stop=True)
            nc.scalar.copy(out=hidden_bias[:], in_=bank[:])

        def finish_chunk(n, sums):
            for t in range(2):
                nc.vector.tensor_tensor(out=biased[n][t][:], in0=sums[t], in1=chunk_bias[n], op=ALU.add)
                if n == 2:
                    nc.scalar.activation(
                        out=h_rows[t][:, B:], in_=biased[n][t][:], func=ACT.Relu, scale=takes[:, 0, t : t + 1]
                    )

        def select_first_half():
            for t in range(2):
                part1 = part_pool.tile([P, B], BF16, tag="part1")
                part2 = part_pool.tile([P, B], BF16, tag="part2")
                for part, n, branch in ((part1, 1, 0), (part2, 0, 1)):
                    nc.vector.tensor_scalar(
                        out=part[:], in0=biased[n][t][:], scalar1=0.0, scalar2=takes[:, branch, t : t + 1], op0=ALU.max, op1=ALU.mult
                    )
                nc.vector.tensor_tensor(out=h_rows[t][:, 0:B], in0=part1[:], in1=part2[:], op=ALU.add)

        def nothing():
            return None

        x_items = []
        for g in range(X_GROUPS):
            cols = slice(g * GROUP_COLS, (g + 1) * GROUP_COLS)
            turn, quantise = turned_group(stepped(pass_words(x_rows[g][:])), False, 4 if g < 2 else 3, x_codes[:, cols], x_scales[:, cols])
            x_items.append((nothing, turn, quantise, nothing))

        w_items = []
        for n in range(W_CHUNKS):
            open_sums = []
            for q in range(CHUNK_GROUPS):
                w = n * CHUNK_GROUPS + q
                codes = codes_pool.tile([P, GROUP_COLS], U32, tag="codes", align_bytes=64)
                scales = codes_pool.tile([P, GROUP_COLS], U8, tag="scales", align_bytes=64)
                if w in STEPPED:
                    passes = [words for rows in w_rows[w] for words in pass_words(rows)]
                    sort, blocks = nothing, stepped([passes[a * BANKS + i] for i in range(BANKS) for a in range(2)])
                else:
                    sort, blocks = presorted(w_rows[w], [a * BANKS + i for i in range(BANKS) for a in range(2)], nc.vector.tensor_copy)
                turn, quantise = turned_group(blocks, False, 2 if w < 4 else 1 if w == 4 else 0, codes[:], scales[:])

                def multiply(w=w, n=n, q=q, codes=codes, scales=scales, open_sums=open_sums):
                    for t in range(2):
                        if q == 0:
                            sums = sums_pool.tile([P, N_OUT], F32, tag="sums")
                            open_sums.append(sums[:, 0:B])
                        for j in range(BANKS):
                            g = q * BANKS + j
                            first = ((g // HALF_PASSES * 2 + t) * HALF_PASSES + g % HALF_PASSES) * P
                            nc.tensor.matmul_mx(
                                out=open_sums[t],
                                lhsT=x_codes[:, first : first + P].bitcast(FP8X4),
                                lhsT_scale=x_scales[:, first : first + P],
                                rhs=codes[:, j * B : (j + 1) * B].bitcast(FP8X4),
                                rhs_scale=scales[:, j * B : (j + 1) * B],
                                start=(g == 0),
                                stop=(g == PASSES - 1),
                            )
                    if q == CHUNK_GROUPS - 1:
                        finish_chunk(n, open_sums)
                    if w == 8:
                        compare_means()
                    if w == 9:
                        select_first_half()

                w_items.append((sort, turn, quantise, multiply))

        def turn_h():
            bank = psum.tile([P, 4, P], F32, tag="bank")
            for t in range(2):
                for u in range(2):
                    nc.tensor.transpose(bank[:, 2 * t + u, :], h_rows[t][:].bitcast(F32)[:, u:PASS_WORDS:2], ident_f32[:])
            nc.vector.tensor_copy(
                out=h_grouped[:].bitcast(F32).rearrange("p (t r u) -> p t r u", t=2, u=2),
                in_=bank[:].rearrange("p (t u) r -> p t r u", u=2),
            )
            nc.vector.quantize_mx(out=h_codes[:].bitcast(FP8X4), scales=h_scales[:], in_=h_grouped[:])

        f_items = []
        for c, (start, width) in enumerate(f_spans):
            codes = codes_pool.tile([P, GROUP_COLS], U32, tag="codes", align_bytes=64)
            scales = codes_pool.tile([P, GROUP_COLS], U8, tag="scales", align_bytes=64)
            if c in F_SORTED:
                sort, blocks = presorted([f_rows[c][:]], range(2 * BANKS), nc.vector.tensor_copy)
            else:
                sort, blocks = nothing, stepped(pass_words(f_rows[c][:, 0 : 4 * width]))
            turn, quantise = turned_group(blocks, True, 0, codes[:, 0:width], scales[:, 0:width], width // B)

            def multiply(c=c, start=start, width=width, codes=codes, scales=scales):
                for t in range(2):
                    result = out_pool.tile([P, GROUP_COLS], F32, tag="result")
                    for j in range(width // N_OUT):
                        cols = slice(j * N_OUT, (j + 1) * N_OUT)
                        if j == 0:
                            sums = sums_pool.tile([P, N_OUT], F32, tag="sums")
                        else:
                            sums = psum.tile([P, N_OUT], F32, tag="bank")
                        nc.tensor.matmul_mx(
                            out=sums[:],
                            lhsT=h_codes[:, t * P : (t + 1) * P].bitcast(FP8X4),
                            lhsT_scale=h_scales[:, t * P : (t + 1) * P],
                            rhs=codes[:, cols].bitcast(FP8X4),
                            rhs_scale=scales[:, cols],
                            start=True,
                            stop=True,
                        )
                        first = start + j * N_OUT
                        if t == 0 and j == 0 and c < 8:
                            nc.scalar.copy(out=result[:, cols], in_=sums[:])
                            nc.gpsimd.tensor_tensor(
                                out=result[:, cols], in0=result[:, cols], in1=bias[:, first : first + N_OUT], op=ALU.add
                            )
                        else:
                            nc.vector.tensor_tensor(
                                out=result[:, cols], in0=sums[:], in1=bias[:, first : first + N_OUT], op=ALU.add
                            )
                    nc.sync.dma_start(out=out[t * P : (t + 1) * P, start : start + width], in_=result[:, 0:width])

            f_items.append((sort, turn, quantise, multiply))

        items = x_items[0:2] + w_items[0:2] + x_items[2:4] + w_items[2:] + [(nothing, nothing, nothing, turn_h)] + f_items
        for i in range(len(items) + 2):
            for piece in {0: (0, 1), 1: (2, 3), 2: (4, 5), 3: (6, 7), 4: (8,), 5: (9, 10), 6: (11, 12), 7: (13,), 8: (14,), 9: (15,)}.get(i, ()):
                sum_abs(piece)
            if i < len(items):
                items[i][1]()
            if i + 1 < len(items):
                items[i + 1][0]()
            if 1 <= i <= len(items):
                items[i - 1][2]()
            if i >= 2:
                items[i - 2][3]()
            if i == 8:
                spread_hidden_bias()
